import numpy as np
import ml_dtypes


def mxq(x, axis, fmt="e4m3"):
    dtype, down = {"e4m3": (ml_dtypes.float8_e4m3fn, 7), "e5m2": (ml_dtypes.float8_e5m2, 14)}[fmt]
    v = np.moveaxis(np.asarray(x, np.float32).astype(ml_dtypes.bfloat16).astype(np.float64), axis, -1)
    blocks = v.reshape(v.shape[:-1] + (-1, 32))
    amax = np.abs(blocks).max(-1, keepdims=True)
    byte = np.maximum(np.where(amax > 0, np.frexp(amax)[1] - 1 + 127, 0) - down, 1)
    scale = np.exp2(byte - 127.0)
    codes = (blocks / scale).astype(np.float32).astype(dtype).astype(np.float64)
    return np.moveaxis((codes * scale).reshape(v.shape), -1, axis)


WIDE = False


def mx_kscale(k):
    if not WIDE:
        return np.ones(k)
    levels = np.array([10, -10, 5, -5, 0])
    a = np.random.permutation(np.resize(levels, k // 512 * 4)).reshape(k // 512, 4)
    idx = np.arange(k)
    return np.exp2(a[idx // 512, idx % 128 // 32])


BF16 = ml_dtypes.bfloat16


def bf(x):
    return np.asarray(x, np.float32).astype(BF16)


def f64(x):
    return np.asarray(x).astype(np.float64)


B, L, D, DE, G, C, O = 4, 128, 1024, 16384, 8, 64, 1024
GD = DE // G
CG = C * G
LG = L * G
EPS_BN = 1e-5
EPS_L2 = 1e-12


def sigmoid(v):
    return 1.0 / (1.0 + np.exp(-v))


def setup_inputs():
    s = mx_kscale(DE)
    cs = s.reshape(G, GD).max(axis=0)
    return {"xe": bf(np.random.standard_normal((B, L, DE)) * s),
            "Ws": bf(np.random.standard_normal((CG, DE)) / np.sqrt(DE) / s),
            "bn1_g": bf(1.0 + 0.1 * np.random.standard_normal(C)),
            "bn1_b": bf(0.1 * np.random.standard_normal(C)),
            "att_lin": bf(np.random.standard_normal((B, L, G))),
            "ba": bf(0.1 * np.random.standard_normal(G)),
            "centroids": bf(np.random.uniform(0.0, 1.0, (C, GD)) * 4.0 / np.sqrt(LG) * cs)}


def reference(xe, Ws, bn1_g, bn1_b, att_lin, ba, centroids):
    xe = f64(xe)
    sa = mxq(xe, 2, "e4m3") @ mxq(f64(Ws), 1, "e4m3").T
    t = sa.reshape(-1, C)
    mu = t.mean(axis=0)
    var = t.var(axis=0)
    t = (t - mu) / np.sqrt(var + EPS_BN) * f64(bn1_g) + f64(bn1_b)
    z = t.reshape(B, L, C, G)
    e = np.exp(z - z.max(axis=2, keepdims=True))
    soft = e / e.sum(axis=2, keepdims=True)
    att = sigmoid(f64(att_lin) + f64(ba))
    act = att[:, :, None, :] * soft
    a_sum = act.sum(axis=(1, 3))
    second = a_sum[:, :, None] * f64(centroids)[None, :, :]
    act_t = act.transpose(0, 2, 1, 3).reshape(B, C, LG)
    xg = xe.reshape(B, LG, GD)
    first = mxq(act_t, 2, "e4m3") @ mxq(xg, 1, "e4m3")
    vlad = first - second
    n = np.sqrt((vlad * vlad).sum(axis=2, keepdims=True))
    return vlad / np.maximum(n, EPS_L2)

@@ -1,0 +1,353 @@
+from contextlib import ExitStack
+
+import concourse.mybir as mybir
+from concourse.masks import make_identity
+
+F32 = mybir.dt.float32
+BF16 = mybir.dt.bfloat16
+U32 = mybir.dt.uint32
+U8 = mybir.dt.uint8
+I32 = mybir.dt.int32
+FP8X4 = mybir.dt.float8_e4m3fn_x4
+ALU = mybir.AluOpType
+ACT = mybir.ActivationFunctionType
+AXIS = mybir.AxisListType
+
+P = 128
+PACK = 4
+K_PASS = P * PACK
+BANK = 512
+
+CLIPS, FRAMES, FEATURES, GROUPS, CLUSTERS = 4, 128, 16384, 8, 64
+GROUP_WIDTH = FEATURES // GROUPS
+LOGITS = CLUSTERS * GROUPS
+ROWS = CLIPS * FRAMES
+LOGIT_TILES = LOGITS // P
+EPS_BN = 1e-5
+EPS_L2 = 1e-12
+
+PIECE_D = 1024
+PIECE = PACK * PIECE_D
+PIECE_PASSES = PIECE // K_PASS
+CHUNKS = FEATURES // PIECE
+GROUP_HALVES = GROUPS // PACK
+D_PARTS = GROUP_WIDTH // PIECE_D
+BANK_PASSES = 2
+D_BANKS = GROUP_WIDTH // BANK
+
+VECTOR_D = 768
+
+FLOPS = 2 * ROWS * LOGITS * FEATURES + 2 * CLIPS * CLUSTERS * FRAMES * GROUPS * GROUP_WIDTH
+
+
+def load_piece(nc, raw_pool, rows, chunk):
+    half, part = divmod(chunk, D_PARTS)
+    raw = raw_pool.tile([P, PIECE], BF16, tag="raw")
+    nc.sync.dma_start(
+        out=raw[:].rearrange("p (j d) -> p j d", j=PACK),
+        in_=rows.rearrange("r (g d) -> r g d", g=GROUPS)[
+            :, PACK * half : PACK * (half + 1), PIECE_D * part : PIECE_D * (part + 1)
+        ],
+    )
+    return raw
+
+
+def transpose_piece(nc, psum_tmp, grouped_pool, identity, raw):
+    words = raw[:].bitcast(F32)
+    grouped = grouped_pool.tile([P, PIECE_PASSES * P * PACK], BF16, tag="grouped", align_bytes=64)
+    grouped_words = grouped[:].bitcast(F32).rearrange("p (k r u) -> p k r u", k=PIECE_PASSES, u=2)
+    for q in range(PIECE_PASSES // BANK_PASSES):
+        bank = psum_tmp.tile([P, BANK_PASSES, 2, P], F32, tag="tmp")
+        for k in range(BANK_PASSES):
+            for u in range(2):
+                word = (K_PASS // 2) * (BANK_PASSES * q + k) + P * u
+                nc.tensor.transpose(bank[:, k, u, :], words[:, word : word + P], identity[:])
+        nc.scalar.copy(
+            out=grouped_words[:, BANK_PASSES * q : BANK_PASSES * (q + 1), :, :],
+            in_=bank[:].rearrange("p k u r -> p k r u"),
+        )
+    return grouped
+
+
+def quantise_frames(nc, grouped, codes, scales, clip):
+    cols = slice(P * clip, P * (clip + 1))
+    for k in range(PIECE_PASSES):
+        nc.vector.quantize_mx(
+            out=codes[:, k, cols].bitcast(FP8X4),
+            scales=scales[:, k, cols],
+            in_=grouped[:, K_PASS * k : K_PASS * (k + 1)],
+        )
+
+
+def quantise_weights(nc, grouped, codes, scales):
+    width = BANK_PASSES * P
+    for q in range(PIECE_PASSES // BANK_PASSES):
+        nc.vector.quantize_mx(
+            out=codes[:, width * q : width * (q + 1)].bitcast(FP8X4),
+            scales=scales[:, width * q : width * (q + 1)],
+            in_=grouped[:, PACK * width * q : PACK * width * (q + 1)],
+        )
+
+
+def quantise_for_aggregation(nc, side_pool, raw, codes, scales):
+    side = side_pool.tile([P, PIECE_D, PACK], BF16, tag="side", align_bytes=64)
+    dst = side[:].rearrange("p (c i) j -> p c j i", i=4)
+    src = raw[:].rearrange("p (j c i) -> p c j i", j=PACK, i=4)
+    cut = VECTOR_D // 4
+    nc.vector.tensor_copy(out=dst[:, 0:cut], in_=src[:, 0:cut])
+    nc.scalar.copy(out=dst[:, cut:], in_=src[:, cut:])
+    nc.vector.quantize_mx(
+        out=codes.bitcast(FP8X4),
+        scales=scales,
+        in_=side[:].rearrange("p d j -> p (d j)"),
+    )
+
+
+def tile_netxtvladconsensus_pa_k_kernel(tc, xe, Ws, bn1_g, bn1_b, att_lin, ba, centroids, out):
+    nc = tc.nc
+    with ExitStack() as ctx:
+        keep = ctx.enter_context(tc.tile_pool(name="keep", bufs=1))
+        psum_acc = ctx.enter_context(tc.psum_pool(name="psum_acc", bufs=4))
+        psum_tmp = ctx.enter_context(tc.psum_pool(name="psum_tmp", bufs=4))
+
+        identity = keep.tile([P, P], F32)
+        make_identity(nc, identity[:])
+        pair_sum = keep.tile([P, P], F32)
+        pair_diff = keep.tile([P, P], F32)
+        lo, hi = slice(0, P // 2), slice(P // 2, P)
+        nc.vector.tensor_add(out=pair_sum[:, lo], in0=identity[:, lo], in1=identity[:, hi])
+        nc.vector.tensor_add(out=pair_sum[:, hi], in0=identity[:, lo], in1=identity[:, hi])
+        nc.vector.tensor_sub(out=pair_diff[:, lo], in0=identity[:, lo], in1=identity[:, hi])
+        nc.vector.tensor_sub(out=pair_diff[:, hi], in0=identity[:, hi], in1=identity[:, lo])
+        ones = keep.tile([P, 2], F32)
+        nc.vector.memset(ones[:], 1.0)
+        minus_half = keep.tile([P, 1], F32)
+        nc.vector.memset(minus_half[:], -0.5)
+
+        gb_rows = keep.tile([P, P], BF16)
+        nc.vector.memset(gb_rows[:], 0.0)
+        for row, vector in enumerate((bn1_g, bn1_b)):
+            for cols in (lo, hi):
+                nc.scalar.dma_start(out=gb_rows[row : row + 1, cols], in_=vector.rearrange("(o c) -> o c", o=1))
+        gb_rows32 = keep.tile([P, P], F32)
+        nc.vector.tensor_copy(out=gb_rows32[:], in_=gb_rows[:])
+        gb_ps = psum_tmp.tile([P, P], F32, tag="tmp")
+        nc.tensor.transpose(gb_ps[:], gb_rows32[:], identity[:])
+        gains = keep.tile([P, 2], F32)
+        nc.vector.tensor_copy(out=gains[:, 0:1], in_=gb_ps[:, 0:1])
+        nc.vector.tensor_scalar_mul(out=gains[:, 1:2], in0=gb_ps[:, 0:1], scalar1=-1.0)
+        bn_bias = keep.tile([P, 1], F32)
+        nc.vector.tensor_copy(out=bn_bias[:], in_=gb_ps[:, 1:2])
+
+        att_raw = keep.tile([P, CLIPS, GROUPS], BF16)
+        nc.scalar.dma_start(out=att_raw[:], in_=att_lin.rearrange("b l g -> l b g"))
+        ba_all = keep.tile([P, GROUPS], BF16)
+        nc.scalar.dma_start(out=ba_all[:], in_=ba.partition_broadcast(P))
+        att = keep.tile([P, CLIPS, GROUPS], F32)
+        nc.vector.tensor_tensor(
+            out=att[:], in0=att_raw[:], in1=ba_all[:].unsqueeze(1).to_broadcast([P, CLIPS, GROUPS]), op=ALU.add
+        )
+        nc.scalar.activation(out=att[:], in_=att[:], func=ACT.Sigmoid)
+        table_warm = keep.tile([P, 1], F32)
+        nc.scalar.activation(out=table_warm[:], in_=att[:, 0, 0:1], func=ACT.Exp)
+
+        agg_codes = keep.tile([P, CLIPS, GROUP_HALVES, GROUP_WIDTH], U32, align_bytes=64)
+        agg_scales = keep.tile([P, CLIPS, GROUP_HALVES, GROUP_WIDTH], U8, align_bytes=64)
+        act_codes = keep.tile([P, CLIPS * GROUP_HALVES * P], U32, align_bytes=64)
+        act_scales = keep.tile([P, CLIPS * GROUP_HALVES * P], U8, align_bytes=64)
+        nc.vector.memset(act_codes[:].bitcast(I32), 0)
+        nc.vector.memset(act_scales[:].bitcast(I32), 0)
+        act_codes_v = act_codes[:].rearrange("p (b h m) -> p b h m", b=CLIPS, h=GROUP_HALVES)
+        act_scales_v = act_scales[:].rearrange("p (b h m) -> p b h m", b=CLIPS, h=GROUP_HALVES)
+
+        stats = keep.tile([P, LOGIT_TILES, 6], F32)
+
+        logits_t = [psum_acc.tile([P, ROWS], F32, tag="acc", name="logits_t%d" % i) for i in range(LOGIT_TILES)]
+
+        pieces = [("x", 0, clip) for clip in range(CLIPS)]
+        for chunk in range(CHUNKS):
+            for i in range(LOGIT_TILES):
+                pieces.append(("w", chunk, i))
+                if chunk + 1 < CHUNKS:
+                    pieces.append(("x", chunk + 1, i))
+
+        with ExitStack() as stream:
+            raw_pool = stream.enter_context(tc.tile_pool(name="raw", bufs=6))
+            grouped_pool = stream.enter_context(tc.tile_pool(name="grouped", bufs=3))
+            side_pool = stream.enter_context(tc.tile_pool(name="side", bufs=2))
+            frames_pool = stream.enter_context(tc.tile_pool(name="frames", bufs=2))
+            weights_pool = stream.enter_context(tc.tile_pool(name="weights", bufs=3))
+
+            raws, groupeds, frame_ops, weight_ops = {}, {}, {}, {}
+            for step in range(len(pieces) + 2):
+                if step < len(pieces):
+                    kind, chunk, index = pieces[step]
+                    rows = xe[index] if kind == "x" else Ws[P * index : P * (index + 1), :]
+                    raws[step] = load_piece(nc, raw_pool, rows, chunk)
+                    groupeds[step] = transpose_piece(nc, psum_tmp, grouped_pool, identity, raws[step])
+                if 1 <= step <= len(pieces):
+                    kind, chunk, index = pieces[step - 1]
+                    if kind == "x":
+                        if index == 0:
+                            x_codes = frames_pool.tile([P, PIECE_PASSES, ROWS], U32, tag="x_codes", align_bytes=64)
+                            x_scales = frames_pool.tile([P, PIECE_PASSES, ROWS], U8, tag="x_scales", align_bytes=64)
+                            frame_ops[chunk] = (x_codes, x_scales)
+                        x_codes, x_scales = frame_ops[chunk]
+                        quantise_frames(nc, groupeds[step - 1], x_codes, x_scales, index)
+                        half, part = divmod(chunk, D_PARTS)
+                        d_cols = slice(PIECE_D * part, PIECE_D * (part + 1))
+                        quantise_for_aggregation(
+                            nc, side_pool, raws[step - 1], agg_codes[:, index, half, d_cols], agg_scales[:, index, half, d_cols]
+                        )
+                    else:
+                        w_codes = weights_pool.tile([P, PIECE_PASSES * P], U32, tag="w_codes", align_bytes=64)
+                        w_scales = weights_pool.tile([P, PIECE_PASSES * P], U8, tag="w_scales", align_bytes=64)
+                        weight_ops[step - 1] = (w_codes, w_scales)
+                        quantise_weights(nc, groupeds[step - 1], w_codes, w_scales)
+                if step >= 2 and pieces[step - 2][0] == "w":
+                    kind, chunk, index = pieces[step - 2]
+                    w_codes, w_scales = weight_ops[step - 2]
+                    x_codes, x_scales = frame_ops[chunk]
+                    for k in range(PIECE_PASSES):
+                        nc.tensor.matmul_mx(
+                            out=logits_t[index][:],
+                            lhsT=w_codes[:, P * k : P * (k + 1)].bitcast(FP8X4),
+                            lhsT_scale=w_scales[:, P * k : P * (k + 1)],
+                            rhs=x_codes[:, k, :].bitcast(FP8X4),
+                            rhs_scale=x_scales[:, k, :],
+                            start=(chunk == 0 and k == 0),
+                            stop=(chunk == CHUNKS - 1 and k == PIECE_PASSES - 1),
+                        )
+                    if chunk == CHUNKS - 1:
+                        nc.vector.bn_stats(out=stats[:, index, :], in_=logits_t[index][:])
+
+        tail = ctx.enter_context(tc.tile_pool(name="tail", bufs=2))
+
+        cent = tail.tile([P, GROUP_WIDTH], BF16, bufs=1)
+        nc.sync.dma_start(out=cent[lo, :], in_=centroids)
+        nc.scalar.dma_start(out=cent[hi, :], in_=centroids)
+
+        mean_var = tail.tile([P, 2], F32)
+        nc.vector.bn_aggr(out=mean_var[:], in_=stats[:].rearrange("p i s -> p (i s)"))
+        both_ps = psum_tmp.tile([P, 4], F32, tag="tmp")
+        nc.tensor.matmul(both_ps[:, 0:2], lhsT=pair_sum[:], rhs=mean_var[:], start=True, stop=True)
+        nc.tensor.matmul(both_ps[:, 2:4], lhsT=pair_diff[:], rhs=mean_var[:], start=True, stop=True)
+        halves = tail.tile([P, 4], F32)
+        nc.vector.tensor_scalar_mul(out=halves[:], in0=both_ps[:], scalar1=0.5)
+        variance = tail.tile([P, 1], F32)
+        nc.vector.scalar_tensor_tensor(
+            out=variance[:], in0=halves[:, 2:3], scalar=halves[:, 2:3], in1=halves[:, 1:2], op0=ALU.mult, op1=ALU.add
+        )
+        nc.vector.tensor_scalar_add(out=variance[:], in0=variance[:], scalar1=EPS_BN)
+        rstd = tail.tile([P, 1], F32)
+        nc.gpsimd.tensor_tensor(out=rstd[:], in0=variance[:], in1=minus_half[:], op=ALU.pow)
+        slopes = tail.tile([P, 2], F32)
+        nc.vector.tensor_scalar_mul(out=slopes[:], in0=gains[:], scalar1=rstd[:, 0:1])
+        shift = tail.tile([P, 1], F32)
+        nc.vector.scalar_tensor_tensor(
+            out=shift[:], in0=halves[:, 0:1], scalar=slopes[:, 1:2], in1=bn_bias[:], op0=ALU.mult, op1=ALU.add
+        )
+        normed_t = []
+        for i in range(LOGIT_TILES):
+            normed = tail.tile([P, ROWS], F32, name="normed%d" % i, bufs=1)
+            if i % 2 == 0:
+                nc.scalar.activation(
+                    out=normed[:], in_=logits_t[i][:], func=ACT.Identity, bias=shift[:, 0:1], scale=slopes[:, 0:1]
+                )
+            else:
+                nc.vector.tensor_scalar(
+                    out=normed[:], in0=logits_t[i][:], scalar1=slopes[:, 0:1], scalar2=shift[:, 0:1],
+                    op0=ALU.mult, op1=ALU.add,
+                )
+            normed_t.append(normed)
+
+        z_banks = []
+        for clip in range(CLIPS):
+            z = psum_tmp.tile([P, LOGIT_TILES, P], F32, tag="tmp", name="z%d" % clip)
+            for i in range(LOGIT_TILES):
+                nc.tensor.transpose(z[:, i, :], normed_t[i][:, P * clip : P * (clip + 1)], identity[:])
+            z_banks.append(z)
+
+        out_rows = out.rearrange("b c d -> (b c) d")
+        for pair in range(CLIPS // 2):
+            frame_sums = tail.tile([P, P], F32, tag="frame_sums")
+            bank_pool, bank_tag = (psum_acc, "acc") if pair == 0 else (psum_tmp, "tmp")
+            small_pool, small_tag = (psum_tmp, "tmp") if pair == 0 else (psum_acc, "acc")
+            first = [bank_pool.tile([P, BANK], F32, tag=bank_tag, name="first%d_%d" % (pair, n)) for n in range(D_BANKS)]
+            for side_of_pair in range(2):
+                clip = 2 * pair + side_of_pair
+                cols = slice(CLUSTERS * side_of_pair, CLUSTERS * (side_of_pair + 1))
+                z_gc = z_banks[clip][:].rearrange("p i k -> p (i k)").rearrange("p (c g) -> p g c", g=GROUPS)
+                neg_max = tail.tile([P, GROUPS], F32, tag="neg_max")
+                nc.vector.tensor_reduce(out=neg_max[:], in_=z_gc, axis=AXIS.X, op=ALU.max, negate=True)
+                expo = tail.tile([P, GROUPS, CLUSTERS], F32, tag="expo")
+                sums = tail.tile([P, GROUPS], F32, tag="sums")
+                for g in range(GROUPS):
+                    nc.scalar.activation(
+                        out=expo[:, g, :], in_=z_gc[:, g, :], func=ACT.Exp, bias=neg_max[:, g : g + 1], scale=1.0,
+                        accum_out=sums[:, g : g + 1],
+                    )
+                weight = tail.tile([P, GROUPS], F32, tag="weight")
+                nc.vector.reciprocal(out=weight[:], in_=sums[:])
+                nc.vector.tensor_mul(out=weight[:], in0=weight[:], in1=att[:, clip, :])
+                act16 = tail.tile([P, GROUP_HALVES, CLUSTERS, PACK], BF16, tag="act16", align_bytes=64)
+                nc.vector.tensor_tensor(
+                    out=act16[:],
+                    in0=expo[:].rearrange("p (h j) c -> p h c j", j=PACK),
+                    in1=weight[:].rearrange("p (h j) -> p h j", j=PACK).unsqueeze(2).to_broadcast(
+                        [P, GROUP_HALVES, CLUSTERS, PACK]
+                    ),
+                    op=ALU.mult,
+                )
+                for half in range(GROUP_HALVES):
+                    nc.vector.quantize_mx(
+                        out=act_codes_v[:, clip, half, cols].bitcast(FP8X4),
+                        scales=act_scales_v[:, clip, half, cols],
+                        in_=act16[:, half].rearrange("p c j -> p (c j)"),
+                    )
+                for n in range(D_BANKS):
+                    for half in range(GROUP_HALVES):
+                        nc.tensor.matmul_mx(
+                            out=first[n][:],
+                            lhsT=act_codes_v[:, clip, half, :].bitcast(FP8X4),
+                            lhsT_scale=act_scales_v[:, clip, half, :],
+                            rhs=agg_codes[:, clip, half, BANK * n : BANK * (n + 1)].bitcast(FP8X4),
+                            rhs_scale=agg_scales[:, clip, half, BANK * n : BANK * (n + 1)],
+                            start=(side_of_pair == 0 and half == 0),
+                            stop=(side_of_pair == 1 and half == GROUP_HALVES - 1),
+                        )
+                act32 = tail.tile([P, GROUPS, CLUSTERS], F32, tag="act32")
+                nc.vector.tensor_tensor(
+                    out=act32[:], in0=expo[:], in1=weight[:].unsqueeze(2).to_broadcast([P, GROUPS, CLUSTERS]), op=ALU.mult
+                )
+                nc.vector.tensor_reduce(
+                    out=frame_sums[:, cols], in_=act32[:].rearrange("p g c -> p c g"), axis=AXIS.X, op=ALU.add
+                )
+
+            a_ps = small_pool.tile([P, 2], F32, tag=small_tag)
+            nc.tensor.matmul(a_ps[:], lhsT=frame_sums[:], rhs=ones[:], start=True, stop=True)
+            neg_a = tail.tile([P, 1], F32, tag="neg_a")
+            nc.vector.tensor_scalar_mul(out=neg_a[:], in0=a_ps[:, 0:1], scalar1=-1.0)
+
+            vlad = tail.tile([P, GROUP_WIDTH], F32, tag="vlad")
+            squares = tail.tile([P, D_BANKS], F32, tag="squares")
+            for n in range(D_BANKS):
+                d_cols = slice(BANK * n, BANK * (n + 1))
+                nc.vector.scalar_tensor_tensor(
+                    out=vlad[:, d_cols], in0=cent[:, d_cols], scalar=neg_a[:, 0:1], in1=first[n][:],
+                    op0=ALU.mult, op1=ALU.add,
+                )
+                squared = tail.tile([P, BANK], F32, tag="squared")
+                nc.scalar.activation(
+                    out=squared[:], in_=vlad[:, d_cols], func=ACT.Square, accum_out=squares[:, n : n + 1]
+                )
+            norm2 = tail.tile([P, 1], F32, tag="norm2")
+            nc.vector.tensor_reduce(out=norm2[:], in_=squares[:], axis=AXIS.X, op=ALU.add)
+            nc.vector.tensor_scalar_max(out=norm2[:], in0=norm2[:], scalar1=EPS_L2 * EPS_L2)
+            inv_norm = tail.tile([P, 1], F32, tag="inv_norm")
+            nc.gpsimd.tensor_tensor(out=inv_norm[:], in0=norm2[:], in1=minus_half[:], op=ALU.pow)
+            left, right = slice(0, GROUP_WIDTH // 2), slice(GROUP_WIDTH // 2, GROUP_WIDTH)
+            nc.vector.tensor_scalar_mul(out=vlad[:, left], in0=vlad[:, left], scalar1=inv_norm[:, 0:1])
+            nc.sync.dma_start(out=out_rows[P * pair : P * (pair + 1), left], in_=vlad[:, left])
+            nc.scalar.activation(out=vlad[:, right], in_=vlad[:, right], func=ACT.Copy, scale=inv_norm[:, 0:1])
+            nc.sync.dma_start(out=out_rows[P * pair : P * (pair + 1), right], in_=vlad[:, right])

@@ -35,7 +35,7 @@ D_PARTS = GROUP_WIDTH // PIECE_D
 BANK_PASSES = 2
 D_BANKS = GROUP_WIDTH // BANK
 
-VECTOR_D = 768
+VECTOR_D = 832
 
 FLOPS = 2 * ROWS * LOGITS * FEATURES + 2 * CLIPS * CLUSTERS * FRAMES * GROUPS * GROUP_WIDTH
 
@@ -89,46 +89,60 @@ def quantise_weights(nc, grouped, codes, scales):
         )
 
 
-def quantise_for_aggregation(nc, side_pool, raw, codes, scales):
+def regroup_for_aggregation(nc, side_pool, raw):
     side = side_pool.tile([P, PIECE_D, PACK], BF16, tag="side", align_bytes=64)
     dst = side[:].rearrange("p (c i) j -> p c j i", i=4)
     src = raw[:].rearrange("p (j c i) -> p c j i", j=PACK, i=4)
     cut = VECTOR_D // 4
     nc.vector.tensor_copy(out=dst[:, 0:cut], in_=src[:, 0:cut])
     nc.scalar.copy(out=dst[:, cut:], in_=src[:, cut:])
-    nc.vector.quantize_mx(
-        out=codes.bitcast(FP8X4),
-        scales=scales,
-        in_=side[:].rearrange("p d j -> p (d j)"),
-    )
+    return side
 
 
 def tile_netxtvladconsensus_pa_k_kernel(tc, xe, Ws, bn1_g, bn1_b, att_lin, ba, centroids, out):
     nc = tc.nc
     with ExitStack() as ctx:
+        ctx.enter_context(tc.manual_schedule())
         keep = ctx.enter_context(tc.tile_pool(name="keep", bufs=1))
         psum_acc = ctx.enter_context(tc.psum_pool(name="psum_acc", bufs=4))
         psum_tmp = ctx.enter_context(tc.psum_pool(name="psum_tmp", bufs=4))
+        lo, hi = slice(0, P // 2), slice(P // 2, P)
 
         identity = keep.tile([P, P], F32)
         make_identity(nc, identity[:])
-        pair_sum = keep.tile([P, P], F32)
-        pair_diff = keep.tile([P, P], F32)
-        lo, hi = slice(0, P // 2), slice(P // 2, P)
-        nc.vector.tensor_add(out=pair_sum[:, lo], in0=identity[:, lo], in1=identity[:, hi])
-        nc.vector.tensor_add(out=pair_sum[:, hi], in0=identity[:, lo], in1=identity[:, hi])
-        nc.vector.tensor_sub(out=pair_diff[:, lo], in0=identity[:, lo], in1=identity[:, hi])
-        nc.vector.tensor_sub(out=pair_diff[:, hi], in0=identity[:, hi], in1=identity[:, lo])
         ones = keep.tile([P, 2], F32)
         nc.vector.memset(ones[:], 1.0)
         minus_half = keep.tile([P, 1], F32)
         nc.vector.memset(minus_half[:], -0.5)
+        table_warm = keep.tile([P, 1], F32)
+        nc.scalar.activation(out=table_warm[:], in_=ones[:, 0:1], func=ACT.Exp)
 
         gb_rows = keep.tile([P, P], BF16)
         nc.vector.memset(gb_rows[:], 0.0)
         for row, vector in enumerate((bn1_g, bn1_b)):
             for cols in (lo, hi):
                 nc.scalar.dma_start(out=gb_rows[row : row + 1, cols], in_=vector.rearrange("(o c) -> o c", o=1))
+        att_raw = keep.tile([P, CLIPS, GROUPS], BF16)
+        nc.scalar.dma_start(out=att_raw[:], in_=att_lin.rearrange("b l g -> l b g"))
+        ba_all = keep.tile([P, GROUPS], BF16)
+        nc.scalar.dma_start(out=ba_all[:], in_=ba.partition_broadcast(P))
+
+        agg_codes = keep.tile([P, CLIPS, GROUP_HALVES, GROUP_WIDTH], U32, align_bytes=64)
+        agg_scales = keep.tile([P, CLIPS, GROUP_HALVES, GROUP_WIDTH], U8, align_bytes=64)
+        act_codes = keep.tile([P, CLIPS * GROUP_HALVES * P], U32, align_bytes=64)
+        act_scales = keep.tile([P, CLIPS * GROUP_HALVES * P], U8, align_bytes=64)
+        nc.vector.memset(act_codes[:].bitcast(I32), 0)
+        nc.vector.memset(act_scales[:].bitcast(I32), 0)
+        act_codes_v = act_codes[:].rearrange("p (b h m) -> p b h m", b=CLIPS, h=GROUP_HALVES)
+        act_scales_v = act_scales[:].rearrange("p (b h m) -> p b h m", b=CLIPS, h=GROUP_HALVES)
+
+        pair_sum = keep.tile([P, P], F32)
+        pair_diff = keep.tile([P, P], F32)
+        nc.vector.tensor_add(out=pair_sum[:, lo], in0=identity[:, lo], in1=identity[:, hi])
+        nc.vector.tensor_add(out=pair_sum[:, hi], in0=identity[:, lo], in1=identity[:, hi])
+        nc.vector.tensor_sub(out=pair_diff[:, lo], in0=identity[:, lo], in1=identity[:, hi])
+        nc.vector.tensor_sub(out=pair_diff[:, hi], in0=identity[:, hi], in1=identity[:, lo])
+
         gb_rows32 = keep.tile([P, P], F32)
         nc.vector.tensor_copy(out=gb_rows32[:], in_=gb_rows[:])
         gb_ps = psum_tmp.tile([P, P], F32, tag="tmp")
@@ -139,26 +153,13 @@ def tile_netxtvladconsensus_pa_k_kernel(tc, xe, Ws, bn1_g, bn1_b, att_lin, ba, c
         bn_bias = keep.tile([P, 1], F32)
         nc.vector.tensor_copy(out=bn_bias[:], in_=gb_ps[:, 1:2])
 
-        att_raw = keep.tile([P, CLIPS, GROUPS], BF16)
-        nc.scalar.dma_start(out=att_raw[:], in_=att_lin.rearrange("b l g -> l b g"))
-        ba_all = keep.tile([P, GROUPS], BF16)
-        nc.scalar.dma_start(out=ba_all[:], in_=ba.partition_broadcast(P))
         att = keep.tile([P, CLIPS, GROUPS], F32)
         nc.vector.tensor_tensor(
             out=att[:], in0=att_raw[:], in1=ba_all[:].unsqueeze(1).to_broadcast([P, CLIPS, GROUPS]), op=ALU.add
         )
-        nc.scalar.activation(out=att[:], in_=att[:], func=ACT.Sigmoid)
-        table_warm = keep.tile([P, 1], F32)
-        nc.scalar.activation(out=table_warm[:], in_=att[:, 0, 0:1], func=ACT.Exp)
-
-        agg_codes = keep.tile([P, CLIPS, GROUP_HALVES, GROUP_WIDTH], U32, align_bytes=64)
-        agg_scales = keep.tile([P, CLIPS, GROUP_HALVES, GROUP_WIDTH], U8, align_bytes=64)
-        act_codes = keep.tile([P, CLIPS * GROUP_HALVES * P], U32, align_bytes=64)
-        act_scales = keep.tile([P, CLIPS * GROUP_HALVES * P], U8, align_bytes=64)
-        nc.vector.memset(act_codes[:].bitcast(I32), 0)
-        nc.vector.memset(act_scales[:].bitcast(I32), 0)
-        act_codes_v = act_codes[:].rearrange("p (b h m) -> p b h m", b=CLIPS, h=GROUP_HALVES)
-        act_scales_v = act_scales[:].rearrange("p (b h m) -> p b h m", b=CLIPS, h=GROUP_HALVES)
+        nc.scalar.activation(out=att[:], in_=att[:], func=ACT.Exp, scale=-1.0)
+        nc.vector.tensor_scalar_add(out=att[:], in0=att[:], scalar1=1.0)
+        nc.vector.reciprocal(out=att[:], in_=att[:])
 
         stats = keep.tile([P, LOGIT_TILES, 6], F32)
 
@@ -171,55 +172,68 @@ def tile_netxtvladconsensus_pa_k_kernel(tc, xe, Ws, bn1_g, bn1_b, att_lin, ba, c
                 if chunk + 1 < CHUNKS:
                     pieces.append(("x", chunk + 1, i))
 
+        def kind_of(number):
+            return pieces[number][0] if 0 <= number < len(pieces) else "none"
+
         with ExitStack() as stream:
             raw_pool = stream.enter_context(tc.tile_pool(name="raw", bufs=6))
             grouped_pool = stream.enter_context(tc.tile_pool(name="grouped", bufs=3))
             side_pool = stream.enter_context(tc.tile_pool(name="side", bufs=2))
             frames_pool = stream.enter_context(tc.tile_pool(name="frames", bufs=2))
             weights_pool = stream.enter_context(tc.tile_pool(name="weights", bufs=3))
+            raws, groupeds, sides, frame_ops, weight_ops = {}, {}, {}, {}, {}
 
-            raws, groupeds, frame_ops, weight_ops = {}, {}, {}, {}
-            for step in range(len(pieces) + 2):
-                if step < len(pieces):
+            def multiply(number, passes):
+                chunk, index = pieces[number][1:]
+                w_codes, w_scales = weight_ops[number]
+                x_codes, x_scales = frame_ops[chunk]
+                for k in passes:
+                    nc.tensor.matmul_mx(
+                        out=logits_t[index][:],
+                        lhsT=w_codes[:, P * k : P * (k + 1)].bitcast(FP8X4),
+                        lhsT_scale=w_scales[:, P * k : P * (k + 1)],
+                        rhs=x_codes[:, k, :].bitcast(FP8X4),
+                        rhs_scale=x_scales[:, k, :],
+                        start=(chunk == 0 and k == 0),
+                        stop=(chunk == CHUNKS - 1 and k == PIECE_PASSES - 1),
+                    )
+
+            for step in range(len(pieces) + 3):
+                if kind_of(step) != "none":
                     kind, chunk, index = pieces[step]
                     rows = xe[index] if kind == "x" else Ws[P * index : P * (index + 1), :]
                     raws[step] = load_piece(nc, raw_pool, rows, chunk)
                     groupeds[step] = transpose_piece(nc, psum_tmp, grouped_pool, identity, raws[step])
-                if 1 <= step <= len(pieces):
-                    kind, chunk, index = pieces[step - 1]
-                    if kind == "x":
-                        if index == 0:
-                            x_codes = frames_pool.tile([P, PIECE_PASSES, ROWS], U32, tag="x_codes", align_bytes=64)
-                            x_scales = frames_pool.tile([P, PIECE_PASSES, ROWS], U8, tag="x_scales", align_bytes=64)
-                            frame_ops[chunk] = (x_codes, x_scales)
-                        x_codes, x_scales = frame_ops[chunk]
-                        quantise_frames(nc, groupeds[step - 1], x_codes, x_scales, index)
-                        half, part = divmod(chunk, D_PARTS)
-                        d_cols = slice(PIECE_D * part, PIECE_D * (part + 1))
-                        quantise_for_aggregation(
-                            nc, side_pool, raws[step - 1], agg_codes[:, index, half, d_cols], agg_scales[:, index, half, d_cols]
-                        )
-                    else:
-                        w_codes = weights_pool.tile([P, PIECE_PASSES * P], U32, tag="w_codes", align_bytes=64)
-                        w_scales = weights_pool.tile([P, PIECE_PASSES * P], U8, tag="w_scales", align_bytes=64)
-                        weight_ops[step - 1] = (w_codes, w_scales)
-                        quantise_weights(nc, groupeds[step - 1], w_codes, w_scales)
-                if step >= 2 and pieces[step - 2][0] == "w":
-                    kind, chunk, index = pieces[step - 2]
-                    w_codes, w_scales = weight_ops[step - 2]
-                    x_codes, x_scales = frame_ops[chunk]
-                    for k in range(PIECE_PASSES):
-                        nc.tensor.matmul_mx(
-                            out=logits_t[index][:],
-                            lhsT=w_codes[:, P * k : P * (k + 1)].bitcast(FP8X4),
-                            lhsT_scale=w_scales[:, P * k : P * (k + 1)],
-                            rhs=x_codes[:, k, :].bitcast(FP8X4),
-                            rhs_scale=x_scales[:, k, :],
-                            start=(chunk == 0 and k == 0),
-                            stop=(chunk == CHUNKS - 1 and k == PIECE_PASSES - 1),
-                        )
-                    if chunk == CHUNKS - 1:
-                        nc.vector.bn_stats(out=stats[:, index, :], in_=logits_t[index][:])
+                if kind_of(step - 1) == "x":
+                    chunk, index = pieces[step - 1][1:]
+                    if index == 0:
+                        x_codes = frames_pool.tile([P, PIECE_PASSES, ROWS], U32, tag="x_codes", align_bytes=64)
+                        x_scales = frames_pool.tile([P, PIECE_PASSES, ROWS], U8, tag="x_scales", align_bytes=64)
+                        frame_ops[chunk] = (x_codes, x_scales)
+                    quantise_frames(nc, groupeds[step - 1], frame_ops[chunk][0], frame_ops[chunk][1], index)
+                if kind_of(step - 1) == "w":
+                    w_codes = weights_pool.tile([P, PIECE_PASSES * P], U32, tag="w_codes", align_bytes=64)
+                    w_scales = weights_pool.tile([P, PIECE_PASSES * P], U8, tag="w_scales", align_bytes=64)
+                    weight_ops[step - 1] = (w_codes, w_scales)
+                    quantise_weights(nc, groupeds[step - 1], w_codes, w_scales)
+                if kind_of(step - 2) == "w":
+                    multiply(step - 2, range(PIECE_PASSES // 2, PIECE_PASSES))
+                if kind_of(step - 1) == "w":
+                    multiply(step - 1, range(PIECE_PASSES // 2))
+                if kind_of(step - 1) == "x":
+                    sides[step - 1] = regroup_for_aggregation(nc, side_pool, raws[step - 1])
+                if kind_of(step - 2) == "x":
+                    chunk, index = pieces[step - 2][1:]
+                    half, part = divmod(chunk, D_PARTS)
+                    d_cols = slice(PIECE_D * part, PIECE_D * (part + 1))
+                    nc.vector.quantize_mx(
+                        out=agg_codes[:, index, half, d_cols].bitcast(FP8X4),
+                        scales=agg_scales[:, index, half, d_cols],
+                        in_=sides[step - 2][:].rearrange("p d j -> p (d j)"),
+                    )
+                if kind_of(step - 3) == "w" and pieces[step - 3][1] == CHUNKS - 1:
+                    index = pieces[step - 3][2]
+                    nc.vector.bn_stats(out=stats[:, index, :], in_=logits_t[index][:])
 
         tail = ctx.enter_context(tc.tile_pool(name="tail", bufs=2))
 
@@ -268,12 +282,13 @@ def tile_netxtvladconsensus_pa_k_kernel(tc, xe, Ws, bn1_g, bn1_b, att_lin, ba, c
                 nc.tensor.transpose(z[:, i, :], normed_t[i][:, P * clip : P * (clip + 1)], identity[:])
             z_banks.append(z)
 
-        out_rows = out.rearrange("b c d -> (b c) d")
+        firsts, a_sums = [], []
         for pair in range(CLIPS // 2):
             frame_sums = tail.tile([P, P], F32, tag="frame_sums")
             bank_pool, bank_tag = (psum_acc, "acc") if pair == 0 else (psum_tmp, "tmp")
             small_pool, small_tag = (psum_tmp, "tmp") if pair == 0 else (psum_acc, "acc")
             first = [bank_pool.tile([P, BANK], F32, tag=bank_tag, name="first%d_%d" % (pair, n)) for n in range(D_BANKS)]
+            firsts.append(first)
             for side_of_pair in range(2):
                 clip = 2 * pair + side_of_pair
                 cols = slice(CLUSTERS * side_of_pair, CLUSTERS * (side_of_pair + 1))
@@ -317,24 +332,27 @@ def tile_netxtvladconsensus_pa_k_kernel(tc, xe, Ws, bn1_g, bn1_b, att_lin, ba, c
                             stop=(side_of_pair == 1 and half == GROUP_HALVES - 1),
                         )
                 act32 = tail.tile([P, GROUPS, CLUSTERS], F32, tag="act32")
-                nc.vector.tensor_tensor(
+                nc.gpsimd.tensor_tensor(
                     out=act32[:], in0=expo[:], in1=weight[:].unsqueeze(2).to_broadcast([P, GROUPS, CLUSTERS]), op=ALU.mult
                 )
-                nc.vector.tensor_reduce(
-                    out=frame_sums[:, cols], in_=act32[:].rearrange("p g c -> p c g"), axis=AXIS.X, op=ALU.add
-                )
+                nc.gpsimd.tensor_tensor(out=act32[:, 0:4, :], in0=act32[:, 0:4, :], in1=act32[:, 4:8, :], op=ALU.add)
+                nc.gpsimd.tensor_tensor(out=act32[:, 0:2, :], in0=act32[:, 0:2, :], in1=act32[:, 2:4, :], op=ALU.add)
+                nc.gpsimd.tensor_tensor(out=frame_sums[:, cols], in0=act32[:, 0, :], in1=act32[:, 1, :], op=ALU.add)
 
-            a_ps = small_pool.tile([P, 2], F32, tag=small_tag)
+            a_ps = small_pool.tile([P, 2], F32, tag=small_tag, name="a_ps%d" % pair)
             nc.tensor.matmul(a_ps[:], lhsT=frame_sums[:], rhs=ones[:], start=True, stop=True)
-            neg_a = tail.tile([P, 1], F32, tag="neg_a")
-            nc.vector.tensor_scalar_mul(out=neg_a[:], in0=a_ps[:, 0:1], scalar1=-1.0)
+            a_sums.append(a_ps)
 
+        out_rows = out.rearrange("b c d -> (b c) d")
+        for pair in range(CLIPS // 2):
+            neg_a = tail.tile([P, 1], F32, tag="neg_a")
+            nc.vector.tensor_scalar_mul(out=neg_a[:], in0=a_sums[pair][:, 0:1], scalar1=-1.0)
             vlad = tail.tile([P, GROUP_WIDTH], F32, tag="vlad")
             squares = tail.tile([P, D_BANKS], F32, tag="squares")
             for n in range(D_BANKS):
                 d_cols = slice(BANK * n, BANK * (n + 1))
                 nc.vector.scalar_tensor_tensor(
-                    out=vlad[:, d_cols], in0=cent[:, d_cols], scalar=neg_a[:, 0:1], in1=first[n][:],
+                    out=vlad[:, d_cols], in0=cent[:, d_cols], scalar=neg_a[:, 0:1], in1=firsts[pair][n][:],
                     op0=ALU.mult, op1=ALU.add,
                 )
                 squared = tail.tile([P, BANK], F32, tag="squared")

@@ -35,6 +35,8 @@ D_PARTS = GROUP_WIDTH // PIECE_D
 BANK_PASSES = 2
 D_BANKS = GROUP_WIDTH // BANK
 
+RUN_BANKS = 2
+
 VECTOR_D = 832
 
 FLOPS = 2 * ROWS * LOGITS * FEATURES + 2 * CLIPS * CLUSTERS * FRAMES * GROUPS * GROUP_WIDTH
@@ -52,11 +54,10 @@ def load_piece(nc, raw_pool, rows, chunk):
     return raw
 
 
-def transpose_piece(nc, psum_tmp, grouped_pool, identity, raw):
+def transpose_banks(nc, psum_tmp, identity, raw, grouped, banks):
     words = raw[:].bitcast(F32)
-    grouped = grouped_pool.tile([P, PIECE_PASSES * P * PACK], BF16, tag="grouped", align_bytes=64)
     grouped_words = grouped[:].bitcast(F32).rearrange("p (k r u) -> p k r u", k=PIECE_PASSES, u=2)
-    for q in range(PIECE_PASSES // BANK_PASSES):
+    for q in banks:
         bank = psum_tmp.tile([P, BANK_PASSES, 2, P], F32, tag="tmp")
         for k in range(BANK_PASSES):
             for u in range(2):
@@ -66,7 +67,6 @@ def transpose_piece(nc, psum_tmp, grouped_pool, identity, raw):
             out=grouped_words[:, BANK_PASSES * q : BANK_PASSES * (q + 1), :, :],
             in_=bank[:].rearrange("p k u r -> p k r u"),
         )
-    return grouped
 
 
 def quantise_frames(nc, grouped, codes, scales, clip):
@@ -198,12 +198,15 @@ def tile_netxtvladconsensus_pa_k_kernel(tc, xe, Ws, bn1_g, bn1_b, att_lin, ba, c
                         stop=(chunk == CHUNKS - 1 and k == PIECE_PASSES - 1),
                     )
 
+            runs = PIECE_PASSES // BANK_PASSES // RUN_BANKS
+            share = PIECE_PASSES // 2 // runs
             for step in range(len(pieces) + 3):
                 if kind_of(step) != "none":
                     kind, chunk, index = pieces[step]
                     rows = xe[index] if kind == "x" else Ws[P * index : P * (index + 1), :]
                     raws[step] = load_piece(nc, raw_pool, rows, chunk)
-                    groupeds[step] = transpose_piece(nc, psum_tmp, grouped_pool, identity, raws[step])
+                    grouped = grouped_pool.tile([P, PIECE_PASSES * P * PACK], BF16, tag="grouped", align_bytes=64)
+                    groupeds[step] = grouped
                 if kind_of(step - 1) == "x":
                     chunk, index = pieces[step - 1][1:]
                     if index == 0:
@@ -216,10 +219,15 @@ def tile_netxtvladconsensus_pa_k_kernel(tc, xe, Ws, bn1_g, bn1_b, att_lin, ba, c
                     w_scales = weights_pool.tile([P, PIECE_PASSES * P], U8, tag="w_scales", align_bytes=64)
                     weight_ops[step - 1] = (w_codes, w_scales)
                     quantise_weights(nc, groupeds[step - 1], w_codes, w_scales)
-                if kind_of(step - 2) == "w":
-                    multiply(step - 2, range(PIECE_PASSES // 2, PIECE_PASSES))
-                if kind_of(step - 1) == "w":
-                    multiply(step - 1, range(PIECE_PASSES // 2))
+                for run in range(runs):
+                    if kind_of(step) != "none":
+                        transpose_banks(
+                            nc, psum_tmp, identity, raws[step], groupeds[step], range(RUN_BANKS * run, RUN_BANKS * (run + 1))
+                        )
+                    if kind_of(step - 2) == "w":
+                        multiply(step - 2, range(PIECE_PASSES // 2 + share * run, PIECE_PASSES // 2 + share * (run + 1)))
+                    if kind_of(step - 1) == "w":
+                        multiply(step - 1, range(share * run, share * (run + 1)))
                 if kind_of(step - 1) == "x":
                     sides[step - 1] = regroup_for_aggregation(nc, side_pool, raws[step - 1])
                 if kind_of(step - 2) == "x":

@@ -35,9 +35,9 @@ D_PARTS = GROUP_WIDTH // PIECE_D
 BANK_PASSES = 2
 D_BANKS = GROUP_WIDTH // BANK
 
-RUN_BANKS = 2
-
 VECTOR_D = 832
+LATE_CLIP = CLIPS - 1
+LATE_VECTOR_D = 512
 
 FLOPS = 2 * ROWS * LOGITS * FEATURES + 2 * CLIPS * CLUSTERS * FRAMES * GROUPS * GROUP_WIDTH
 
@@ -54,10 +54,11 @@ def load_piece(nc, raw_pool, rows, chunk):
     return raw
 
 
-def transpose_banks(nc, psum_tmp, identity, raw, grouped, banks):
+def transpose_piece(nc, psum_tmp, grouped_pool, identity, raw):
     words = raw[:].bitcast(F32)
+    grouped = grouped_pool.tile([P, PIECE_PASSES * P * PACK], BF16, tag="grouped", align_bytes=64)
     grouped_words = grouped[:].bitcast(F32).rearrange("p (k r u) -> p k r u", k=PIECE_PASSES, u=2)
-    for q in banks:
+    for q in range(PIECE_PASSES // BANK_PASSES):
         bank = psum_tmp.tile([P, BANK_PASSES, 2, P], F32, tag="tmp")
         for k in range(BANK_PASSES):
             for u in range(2):
@@ -67,6 +68,7 @@ def transpose_banks(nc, psum_tmp, identity, raw, grouped, banks):
             out=grouped_words[:, BANK_PASSES * q : BANK_PASSES * (q + 1), :, :],
             in_=bank[:].rearrange("p k u r -> p k r u"),
         )
+    return grouped
 
 
 def quantise_frames(nc, grouped, codes, scales, clip):
@@ -89,11 +91,11 @@ def quantise_weights(nc, grouped, codes, scales):
         )
 
 
-def regroup_for_aggregation(nc, side_pool, raw):
+def regroup_for_aggregation(nc, side_pool, raw, vector_d):
     side = side_pool.tile([P, PIECE_D, PACK], BF16, tag="side", align_bytes=64)
     dst = side[:].rearrange("p (c i) j -> p c j i", i=4)
     src = raw[:].rearrange("p (j c i) -> p c j i", j=PACK, i=4)
-    cut = VECTOR_D // 4
+    cut = vector_d // 4
     nc.vector.tensor_copy(out=dst[:, 0:cut], in_=src[:, 0:cut])
     nc.scalar.copy(out=dst[:, cut:], in_=src[:, cut:])
     return side
@@ -102,7 +104,6 @@ def regroup_for_aggregation(nc, side_pool, raw):
 def tile_netxtvladconsensus_pa_k_kernel(tc, xe, Ws, bn1_g, bn1_b, att_lin, ba, centroids, out):
     nc = tc.nc
     with ExitStack() as ctx:
-        ctx.enter_context(tc.manual_schedule())
         keep = ctx.enter_context(tc.tile_pool(name="keep", bufs=1))
         psum_acc = ctx.enter_context(tc.psum_pool(name="psum_acc", bufs=4))
         psum_tmp = ctx.enter_context(tc.psum_pool(name="psum_tmp", bufs=4))
@@ -176,6 +177,7 @@ def tile_netxtvladconsensus_pa_k_kernel(tc, xe, Ws, bn1_g, bn1_b, att_lin, ba, c
             return pieces[number][0] if 0 <= number < len(pieces) else "none"
 
         with ExitStack() as stream:
+            stream.enter_context(tc.manual_schedule())
             raw_pool = stream.enter_context(tc.tile_pool(name="raw", bufs=6))
             grouped_pool = stream.enter_context(tc.tile_pool(name="grouped", bufs=3))
             side_pool = stream.enter_context(tc.tile_pool(name="side", bufs=2))
@@ -198,15 +200,12 @@ def tile_netxtvladconsensus_pa_k_kernel(tc, xe, Ws, bn1_g, bn1_b, att_lin, ba, c
                         stop=(chunk == CHUNKS - 1 and k == PIECE_PASSES - 1),
                     )
 
-            runs = PIECE_PASSES // BANK_PASSES // RUN_BANKS
-            share = PIECE_PASSES // 2 // runs
             for step in range(len(pieces) + 3):
                 if kind_of(step) != "none":
                     kind, chunk, index = pieces[step]
                     rows = xe[index] if kind == "x" else Ws[P * index : P * (index + 1), :]
                     raws[step] = load_piece(nc, raw_pool, rows, chunk)
-                    grouped = grouped_pool.tile([P, PIECE_PASSES * P * PACK], BF16, tag="grouped", align_bytes=64)
-                    groupeds[step] = grouped
+                    groupeds[step] = transpose_piece(nc, psum_tmp, grouped_pool, identity, raws[step])
                 if kind_of(step - 1) == "x":
                     chunk, index = pieces[step - 1][1:]
                     if index == 0:
@@ -219,18 +218,13 @@ def tile_netxtvladconsensus_pa_k_kernel(tc, xe, Ws, bn1_g, bn1_b, att_lin, ba, c
                     w_scales = weights_pool.tile([P, PIECE_PASSES * P], U8, tag="w_scales", align_bytes=64)
                     weight_ops[step - 1] = (w_codes, w_scales)
                     quantise_weights(nc, groupeds[step - 1], w_codes, w_scales)
-                for run in range(runs):
-                    if kind_of(step) != "none":
-                        transpose_banks(
-                            nc, psum_tmp, identity, raws[step], groupeds[step], range(RUN_BANKS * run, RUN_BANKS * (run + 1))
-                        )
-                    if kind_of(step - 2) == "w":
-                        multiply(step - 2, range(PIECE_PASSES // 2 + share * run, PIECE_PASSES // 2 + share * (run + 1)))
-                    if kind_of(step - 1) == "w":
-                        multiply(step - 1, range(share * run, share * (run + 1)))
-                if kind_of(step - 1) == "x":
-                    sides[step - 1] = regroup_for_aggregation(nc, side_pool, raws[step - 1])
-                if kind_of(step - 2) == "x":
+                if kind_of(step - 2) == "w":
+                    multiply(step - 2, range(PIECE_PASSES // 2, PIECE_PASSES))
+                if kind_of(step - 1) == "w":
+                    multiply(step - 1, range(PIECE_PASSES // 2))
+                if kind_of(step - 1) == "x" and pieces[step - 1][2] != LATE_CLIP:
+                    sides[step - 1] = regroup_for_aggregation(nc, side_pool, raws[step - 1], VECTOR_D)
+                if kind_of(step - 2) == "x" and pieces[step - 2][2] != LATE_CLIP:
                     chunk, index = pieces[step - 2][1:]
                     half, part = divmod(chunk, D_PARTS)
                     d_cols = slice(PIECE_D * part, PIECE_D * (part + 1))
@@ -243,6 +237,9 @@ def tile_netxtvladconsensus_pa_k_kernel(tc, xe, Ws, bn1_g, bn1_b, att_lin, ba, c
                     index = pieces[step - 3][2]
                     nc.vector.bn_stats(out=stats[:, index, :], in_=logits_t[index][:])
 
+        late_raw_pool = ctx.enter_context(tc.tile_pool(name="late_raw", bufs=CHUNKS))
+        late_side_pool = ctx.enter_context(tc.tile_pool(name="late_side", bufs=2))
+        late_raws = [load_piece(nc, late_raw_pool, xe[LATE_CLIP], chunk) for chunk in range(CHUNKS)]
         tail = ctx.enter_context(tc.tile_pool(name="tail", bufs=2))
 
         cent = tail.tile([P, GROUP_WIDTH], BF16, bufs=1)
@@ -290,66 +287,89 @@ def tile_netxtvladconsensus_pa_k_kernel(tc, xe, Ws, bn1_g, bn1_b, att_lin, ba, c
                 nc.tensor.transpose(z[:, i, :], normed_t[i][:, P * clip : P * (clip + 1)], identity[:])
             z_banks.append(z)
 
-        firsts, a_sums = [], []
-        for pair in range(CLIPS // 2):
-            frame_sums = tail.tile([P, P], F32, tag="frame_sums")
-            bank_pool, bank_tag = (psum_acc, "acc") if pair == 0 else (psum_tmp, "tmp")
-            small_pool, small_tag = (psum_tmp, "tmp") if pair == 0 else (psum_acc, "acc")
-            first = [bank_pool.tile([P, BANK], F32, tag=bank_tag, name="first%d_%d" % (pair, n)) for n in range(D_BANKS)]
-            firsts.append(first)
-            for side_of_pair in range(2):
-                clip = 2 * pair + side_of_pair
-                cols = slice(CLUSTERS * side_of_pair, CLUSTERS * (side_of_pair + 1))
-                z_gc = z_banks[clip][:].rearrange("p i k -> p (i k)").rearrange("p (c g) -> p g c", g=GROUPS)
-                neg_max = tail.tile([P, GROUPS], F32, tag="neg_max")
-                nc.vector.tensor_reduce(out=neg_max[:], in_=z_gc, axis=AXIS.X, op=ALU.max, negate=True)
-                expo = tail.tile([P, GROUPS, CLUSTERS], F32, tag="expo")
-                sums = tail.tile([P, GROUPS], F32, tag="sums")
-                for g in range(GROUPS):
-                    nc.scalar.activation(
-                        out=expo[:, g, :], in_=z_gc[:, g, :], func=ACT.Exp, bias=neg_max[:, g : g + 1], scale=1.0,
-                        accum_out=sums[:, g : g + 1],
-                    )
-                weight = tail.tile([P, GROUPS], F32, tag="weight")
-                nc.vector.reciprocal(out=weight[:], in_=sums[:])
-                nc.vector.tensor_mul(out=weight[:], in0=weight[:], in1=att[:, clip, :])
-                act16 = tail.tile([P, GROUP_HALVES, CLUSTERS, PACK], BF16, tag="act16", align_bytes=64)
-                nc.vector.tensor_tensor(
-                    out=act16[:],
-                    in0=expo[:].rearrange("p (h j) c -> p h c j", j=PACK),
-                    in1=weight[:].rearrange("p (h j) -> p h j", j=PACK).unsqueeze(2).to_broadcast(
-                        [P, GROUP_HALVES, CLUSTERS, PACK]
-                    ),
-                    op=ALU.mult,
-                )
-                for half in range(GROUP_HALVES):
-                    nc.vector.quantize_mx(
-                        out=act_codes_v[:, clip, half, cols].bitcast(FP8X4),
-                        scales=act_scales_v[:, clip, half, cols],
-                        in_=act16[:, half].rearrange("p c j -> p (c j)"),
-                    )
-                for n in range(D_BANKS):
-                    for half in range(GROUP_HALVES):
-                        nc.tensor.matmul_mx(
-                            out=first[n][:],
-                            lhsT=act_codes_v[:, clip, half, :].bitcast(FP8X4),
-                            lhsT_scale=act_scales_v[:, clip, half, :],
-                            rhs=agg_codes[:, clip, half, BANK * n : BANK * (n + 1)].bitcast(FP8X4),
-                            rhs_scale=agg_scales[:, clip, half, BANK * n : BANK * (n + 1)],
-                            start=(side_of_pair == 0 and half == 0),
-                            stop=(side_of_pair == 1 and half == GROUP_HALVES - 1),
-                        )
-                act32 = tail.tile([P, GROUPS, CLUSTERS], F32, tag="act32")
-                nc.gpsimd.tensor_tensor(
-                    out=act32[:], in0=expo[:], in1=weight[:].unsqueeze(2).to_broadcast([P, GROUPS, CLUSTERS]), op=ALU.mult
-                )
-                nc.gpsimd.tensor_tensor(out=act32[:, 0:4, :], in0=act32[:, 0:4, :], in1=act32[:, 4:8, :], op=ALU.add)
-                nc.gpsimd.tensor_tensor(out=act32[:, 0:2, :], in0=act32[:, 0:2, :], in1=act32[:, 2:4, :], op=ALU.add)
-                nc.gpsimd.tensor_tensor(out=frame_sums[:, cols], in0=act32[:, 0, :], in1=act32[:, 1, :], op=ALU.add)
+        firsts = [
+            [psum_acc.tile([P, BANK], F32, tag="acc", name="first0_%d" % n) for n in range(D_BANKS)],
+            [psum_tmp.tile([P, BANK], F32, tag="tmp", name="first1_%d" % n) for n in range(D_BANKS)],
+        ]
+        frame_sums = [tail.tile([P, P], F32, name="frame_sums%d" % pair, bufs=1) for pair in range(CLIPS // 2)]
 
+        def softmax_and_gate(clip):
+            pair, side_of_pair = divmod(clip, 2)
+            cols = slice(CLUSTERS * side_of_pair, CLUSTERS * (side_of_pair + 1))
+            z_gc = z_banks[clip][:].rearrange("p i k -> p (i k)").rearrange("p (c g) -> p g c", g=GROUPS)
+            neg_max = tail.tile([P, GROUPS], F32, tag="neg_max")
+            nc.vector.tensor_reduce(out=neg_max[:], in_=z_gc, axis=AXIS.X, op=ALU.max, negate=True)
+            expo = tail.tile([P, GROUPS, CLUSTERS], F32, tag="expo")
+            sums = tail.tile([P, GROUPS], F32, tag="sums")
+            for g in range(GROUPS):
+                nc.scalar.activation(
+                    out=expo[:, g, :], in_=z_gc[:, g, :], func=ACT.Exp, bias=neg_max[:, g : g + 1], scale=1.0,
+                    accum_out=sums[:, g : g + 1],
+                )
+            weight = tail.tile([P, GROUPS], F32, tag="weight")
+            nc.vector.reciprocal(out=weight[:], in_=sums[:])
+            nc.vector.tensor_mul(out=weight[:], in0=weight[:], in1=att[:, clip, :])
+            act16 = tail.tile([P, GROUP_HALVES, CLUSTERS, PACK], BF16, tag="act16", align_bytes=64)
+            nc.vector.tensor_tensor(
+                out=act16[:],
+                in0=expo[:].rearrange("p (h j) c -> p h c j", j=PACK),
+                in1=weight[:].rearrange("p (h j) -> p h j", j=PACK).unsqueeze(2).to_broadcast(
+                    [P, GROUP_HALVES, CLUSTERS, PACK]
+                ),
+                op=ALU.mult,
+            )
+            for half in range(GROUP_HALVES):
+                nc.vector.quantize_mx(
+                    out=act_codes_v[:, clip, half, cols].bitcast(FP8X4),
+                    scales=act_scales_v[:, clip, half, cols],
+                    in_=act16[:, half].rearrange("p c j -> p (c j)"),
+                )
+            act32 = tail.tile([P, GROUPS, CLUSTERS], F32, tag="act32")
+            nc.gpsimd.tensor_tensor(
+                out=act32[:], in0=expo[:], in1=weight[:].unsqueeze(2).to_broadcast([P, GROUPS, CLUSTERS]), op=ALU.mult
+            )
+            nc.gpsimd.tensor_tensor(out=act32[:, 0:4, :], in0=act32[:, 0:4, :], in1=act32[:, 4:8, :], op=ALU.add)
+            nc.gpsimd.tensor_tensor(out=act32[:, 0:2, :], in0=act32[:, 0:2, :], in1=act32[:, 2:4, :], op=ALU.add)
+            nc.gpsimd.tensor_tensor(out=frame_sums[pair][:, cols], in0=act32[:, 0, :], in1=act32[:, 1, :], op=ALU.add)
+
+        def aggregate(clip):
+            pair, side_of_pair = divmod(clip, 2)
+            for n in range(D_BANKS):
+                for half in range(GROUP_HALVES):
+                    nc.tensor.matmul_mx(
+                        out=firsts[pair][n][:],
+                        lhsT=act_codes_v[:, clip, half, :].bitcast(FP8X4),
+                        lhsT_scale=act_scales_v[:, clip, half, :],
+                        rhs=agg_codes[:, clip, half, BANK * n : BANK * (n + 1)].bitcast(FP8X4),
+                        rhs_scale=agg_scales[:, clip, half, BANK * n : BANK * (n + 1)],
+                        start=(side_of_pair == 0 and half == 0),
+                        stop=(side_of_pair == 1 and half == GROUP_HALVES - 1),
+                    )
+
+        def sum_over_frames(pair, small_pool, small_tag):
             a_ps = small_pool.tile([P, 2], F32, tag=small_tag, name="a_ps%d" % pair)
-            nc.tensor.matmul(a_ps[:], lhsT=frame_sums[:], rhs=ones[:], start=True, stop=True)
-            a_sums.append(a_ps)
+            nc.tensor.matmul(a_ps[:], lhsT=frame_sums[pair][:], rhs=ones[:], start=True, stop=True)
+            return a_ps
+
+        a_sums = []
+        for clip in range(CLIPS):
+            softmax_and_gate(clip)
+            if clip == LATE_CLIP:
+                for chunk in range(CHUNKS):
+                    half, part = divmod(chunk, D_PARTS)
+                    side = regroup_for_aggregation(nc, late_side_pool, late_raws[chunk], LATE_VECTOR_D)
+                    for piece_half in range(2):
+                        d_cols = slice(PIECE_D * part + (PIECE_D // 2) * piece_half, PIECE_D * part + (PIECE_D // 2) * (piece_half + 1))
+                        nc.vector.quantize_mx(
+                            out=agg_codes[:, clip, half, d_cols].bitcast(FP8X4),
+                            scales=agg_scales[:, clip, half, d_cols],
+                            in_=side[:, (PIECE_D // 2) * piece_half : (PIECE_D // 2) * (piece_half + 1), :].rearrange("p d j -> p (d j)"),
+                        )
+            aggregate(clip)
+            if clip == 1:
+                a_sums.append(sum_over_frames(0, psum_tmp, "tmp"))
+            if clip == 3:
+                a_sums.append(sum_over_frames(1, psum_acc, "acc"))
 
         out_rows = out.rearrange("b c d -> (b c) d")
         for pair in range(CLIPS // 2):

@@ -36,7 +36,7 @@ BANK_PASSES = 2
 D_BANKS = GROUP_WIDTH // BANK
 
 VECTOR_D = 832
-LATE_CLIP = CLIPS - 1
+LATE_CHUNK = 0
 LATE_VECTOR_D = 512
 
 FLOPS = 2 * ROWS * LOGITS * FEATURES + 2 * CLIPS * CLUSTERS * FRAMES * GROUPS * GROUP_WIDTH
@@ -222,9 +222,9 @@ def tile_netxtvladconsensus_pa_k_kernel(tc, xe, Ws, bn1_g, bn1_b, att_lin, ba, c
                     multiply(step - 2, range(PIECE_PASSES // 2, PIECE_PASSES))
                 if kind_of(step - 1) == "w":
                     multiply(step - 1, range(PIECE_PASSES // 2))
-                if kind_of(step - 1) == "x" and pieces[step - 1][2] != LATE_CLIP:
+                if kind_of(step - 1) == "x" and pieces[step - 1][1] != LATE_CHUNK:
                     sides[step - 1] = regroup_for_aggregation(nc, side_pool, raws[step - 1], VECTOR_D)
-                if kind_of(step - 2) == "x" and pieces[step - 2][2] != LATE_CLIP:
+                if kind_of(step - 2) == "x" and pieces[step - 2][1] != LATE_CHUNK:
                     chunk, index = pieces[step - 2][1:]
                     half, part = divmod(chunk, D_PARTS)
                     d_cols = slice(PIECE_D * part, PIECE_D * (part + 1))
@@ -237,9 +237,9 @@ def tile_netxtvladconsensus_pa_k_kernel(tc, xe, Ws, bn1_g, bn1_b, att_lin, ba, c
                     index = pieces[step - 3][2]
                     nc.vector.bn_stats(out=stats[:, index, :], in_=logits_t[index][:])
 
-        late_raw_pool = ctx.enter_context(tc.tile_pool(name="late_raw", bufs=CHUNKS))
+        late_raw_pool = ctx.enter_context(tc.tile_pool(name="late_raw", bufs=CLIPS))
         late_side_pool = ctx.enter_context(tc.tile_pool(name="late_side", bufs=2))
-        late_raws = [load_piece(nc, late_raw_pool, xe[LATE_CLIP], chunk) for chunk in range(CHUNKS)]
+        late_raws = [load_piece(nc, late_raw_pool, xe[clip], LATE_CHUNK) for clip in range(CLIPS)]
         tail = ctx.enter_context(tc.tile_pool(name="tail", bufs=2))
 
         cent = tail.tile([P, GROUP_WIDTH], BF16, bufs=1)
@@ -351,20 +351,22 @@ def tile_netxtvladconsensus_pa_k_kernel(tc, xe, Ws, bn1_g, bn1_b, att_lin, ba, c
             nc.tensor.matmul(a_ps[:], lhsT=frame_sums[pair][:], rhs=ones[:], start=True, stop=True)
             return a_ps
 
+        def quantise_late_piece(clip):
+            half, part = divmod(LATE_CHUNK, D_PARTS)
+            side = regroup_for_aggregation(nc, late_side_pool, late_raws[clip], LATE_VECTOR_D)
+            width = PIECE_D // 2
+            for piece_half in range(2):
+                d_cols = slice(PIECE_D * part + width * piece_half, PIECE_D * part + width * (piece_half + 1))
+                nc.vector.quantize_mx(
+                    out=agg_codes[:, clip, half, d_cols].bitcast(FP8X4),
+                    scales=agg_scales[:, clip, half, d_cols],
+                    in_=side[:, width * piece_half : width * (piece_half + 1), :].rearrange("p d j -> p (d j)"),
+                )
+
         a_sums = []
         for clip in range(CLIPS):
             softmax_and_gate(clip)
-            if clip == LATE_CLIP:
-                for chunk in range(CHUNKS):
-                    half, part = divmod(chunk, D_PARTS)
-                    side = regroup_for_aggregation(nc, late_side_pool, late_raws[chunk], LATE_VECTOR_D)
-                    for piece_half in range(2):
-                        d_cols = slice(PIECE_D * part + (PIECE_D // 2) * piece_half, PIECE_D * part + (PIECE_D // 2) * (piece_half + 1))
-                        nc.vector.quantize_mx(
-                            out=agg_codes[:, clip, half, d_cols].bitcast(FP8X4),
-                            scales=agg_scales[:, clip, half, d_cols],
-                            in_=side[:, (PIECE_D // 2) * piece_half : (PIECE_D // 2) * (piece_half + 1), :].rearrange("p d j -> p (d j)"),
-                        )
+            quantise_late_piece(clip)
             aggregate(clip)
             if clip == 1:
                 a_sums.append(sum_over_frames(0, psum_tmp, "tmp"))

@@ -182,7 +182,7 @@ def tile_netxtvladconsensus_pa_k_kernel(tc, xe, Ws, bn1_g, bn1_b, att_lin, ba, c
             grouped_pool = stream.enter_context(tc.tile_pool(name="grouped", bufs=3))
             side_pool = stream.enter_context(tc.tile_pool(name="side", bufs=2))
             frames_pool = stream.enter_context(tc.tile_pool(name="frames", bufs=2))
-            weights_pool = stream.enter_context(tc.tile_pool(name="weights", bufs=3))
+            weights_pool = stream.enter_context(tc.tile_pool(name="weights", bufs=4))
             raws, groupeds, sides, frame_ops, weight_ops = {}, {}, {}, {}, {}
 
             def multiply(number, passes):
@@ -200,7 +200,7 @@ def tile_netxtvladconsensus_pa_k_kernel(tc, xe, Ws, bn1_g, bn1_b, att_lin, ba, c
                         stop=(chunk == CHUNKS - 1 and k == PIECE_PASSES - 1),
                     )
 
-            for step in range(len(pieces) + 3):
+            for step in range(len(pieces) + 4):
                 if kind_of(step) != "none":
                     kind, chunk, index = pieces[step]
                     rows = xe[index] if kind == "x" else Ws[P * index : P * (index + 1), :]
@@ -218,10 +218,10 @@ def tile_netxtvladconsensus_pa_k_kernel(tc, xe, Ws, bn1_g, bn1_b, att_lin, ba, c
                     w_scales = weights_pool.tile([P, PIECE_PASSES * P], U8, tag="w_scales", align_bytes=64)
                     weight_ops[step - 1] = (w_codes, w_scales)
                     quantise_weights(nc, groupeds[step - 1], w_codes, w_scales)
+                if kind_of(step - 3) == "w":
+                    multiply(step - 3, range(PIECE_PASSES // 2, PIECE_PASSES))
                 if kind_of(step - 2) == "w":
-                    multiply(step - 2, range(PIECE_PASSES // 2, PIECE_PASSES))
-                if kind_of(step - 1) == "w":
-                    multiply(step - 1, range(PIECE_PASSES // 2))
+                    multiply(step - 2, range(PIECE_PASSES // 2))
                 if kind_of(step - 1) == "x" and pieces[step - 1][1] != LATE_CHUNK:
                     sides[step - 1] = regroup_for_aggregation(nc, side_pool, raws[step - 1], VECTOR_D)
                 if kind_of(step - 2) == "x" and pieces[step - 2][1] != LATE_CHUNK:
@@ -233,8 +233,8 @@ def tile_netxtvladconsensus_pa_k_kernel(tc, xe, Ws, bn1_g, bn1_b, att_lin, ba, c
                         scales=agg_scales[:, index, half, d_cols],
                         in_=sides[step - 2][:].rearrange("p d j -> p (d j)"),
                     )
-                if kind_of(step - 3) == "w" and pieces[step - 3][1] == CHUNKS - 1:
-                    index = pieces[step - 3][2]
+                if kind_of(step - 4) == "w" and pieces[step - 4][1] == CHUNKS - 1:
+                    index = pieces[step - 4][2]
                     nc.vector.bn_stats(out=stats[:, index, :], in_=logits_t[index][:])
 
         late_raw_pool = ctx.enter_context(tc.tile_pool(name="late_raw", bufs=CLIPS))

@@ -37,7 +37,7 @@ D_BANKS = GROUP_WIDTH // BANK
 
 VECTOR_D = 832
 LATE_CHUNK = 0
-LATE_VECTOR_D = 512
+LATE_VECTOR_D = 384
 
 FLOPS = 2 * ROWS * LOGITS * FEATURES + 2 * CLIPS * CLUSTERS * FRAMES * GROUPS * GROUP_WIDTH
 
@@ -240,7 +240,7 @@ def tile_netxtvladconsensus_pa_k_kernel(tc, xe, Ws, bn1_g, bn1_b, att_lin, ba, c
         late_raw_pool = ctx.enter_context(tc.tile_pool(name="late_raw", bufs=CLIPS))
         late_side_pool = ctx.enter_context(tc.tile_pool(name="late_side", bufs=2))
         late_raws = [load_piece(nc, late_raw_pool, xe[clip], LATE_CHUNK) for clip in range(CLIPS)]
-        tail = ctx.enter_context(tc.tile_pool(name="tail", bufs=2))
+        tail = ctx.enter_context(tc.tile_pool(name="tail", bufs=4))
 
         cent = tail.tile([P, GROUP_WIDTH], BF16, bufs=1)
         nc.sync.dma_start(out=cent[lo, :], in_=centroids)

from contextlib import ExitStack

import concourse.mybir as mybir
from concourse.masks import make_identity

F32 = mybir.dt.float32
BF16 = mybir.dt.bfloat16
U32 = mybir.dt.uint32
U8 = mybir.dt.uint8
I32 = mybir.dt.int32
FP8X4 = mybir.dt.float8_e4m3fn_x4
ALU = mybir.AluOpType
ACT = mybir.ActivationFunctionType
AXIS = mybir.AxisListType

P = 128
PACK = 4
K_PASS = P * PACK
BANK = 512

CLIPS, FRAMES, FEATURES, GROUPS, CLUSTERS = 4, 128, 16384, 8, 64
GROUP_WIDTH = FEATURES // GROUPS
LOGITS = CLUSTERS * GROUPS
ROWS = CLIPS * FRAMES
LOGIT_TILES = LOGITS // P
EPS_BN = 1e-5
EPS_L2 = 1e-12

PIECE_D = 1024
PIECE = PACK * PIECE_D
PIECE_PASSES = PIECE // K_PASS
CHUNKS = FEATURES // PIECE
GROUP_HALVES = GROUPS // PACK
D_PARTS = GROUP_WIDTH // PIECE_D
BANK_PASSES = 2
D_BANKS = GROUP_WIDTH // BANK

VECTOR_D = 832
LATE_CHUNK = 0
LATE_VECTOR_D = 384

FLOPS = 2 * ROWS * LOGITS * FEATURES + 2 * CLIPS * CLUSTERS * FRAMES * GROUPS * GROUP_WIDTH


def load_piece(nc, raw_pool, rows, chunk):
    half, part = divmod(chunk, D_PARTS)
    raw = raw_pool.tile([P, PIECE], BF16, tag="raw")
    nc.sync.dma_start(
        out=raw[:].rearrange("p (j d) -> p j d", j=PACK),
        in_=rows.rearrange("r (g d) -> r g d", g=GROUPS)[
            :, PACK * half : PACK * (half + 1), PIECE_D * part : PIECE_D * (part + 1)
        ],
    )
    return raw


def transpose_piece(nc, psum_tmp, grouped_pool, identity, raw):
    words = raw[:].bitcast(F32)
    grouped = grouped_pool.tile([P, PIECE_PASSES * P * PACK], BF16, tag="grouped", align_bytes=64)
    grouped_words = grouped[:].bitcast(F32).rearrange("p (k r u) -> p k r u", k=PIECE_PASSES, u=2)
    for q in range(PIECE_PASSES // BANK_PASSES):
        bank = psum_tmp.tile([P, BANK_PASSES, 2, P], F32, tag="tmp")
        for k in range(BANK_PASSES):
            for u in range(2):
                word = (K_PASS // 2) * (BANK_PASSES * q + k) + P * u
                nc.tensor.transpose(bank[:, k, u, :], words[:, word : word + P], identity[:])
        nc.scalar.copy(
            out=grouped_words[:, BANK_PASSES * q : BANK_PASSES * (q + 1), :, :],
            in_=bank[:].rearrange("p k u r -> p k r u"),
        )
    return grouped


def quantise_frames(nc, grouped, codes, scales, clip):
    cols = slice(P * clip, P * (clip + 1))
    for k in range(PIECE_PASSES):
        nc.vector.quantize_mx(
            out=codes[:, k, cols].bitcast(FP8X4),
            scales=scales[:, k, cols],
            in_=grouped[:, K_PASS * k : K_PASS * (k + 1)],
        )


def quantise_weights(nc, grouped, codes, scales):
    width = BANK_PASSES * P
    for q in range(PIECE_PASSES // BANK_PASSES):
        nc.vector.quantize_mx(
            out=codes[:, width * q : width * (q + 1)].bitcast(FP8X4),
            scales=scales[:, width * q : width * (q + 1)],
            in_=grouped[:, PACK * width * q : PACK * width * (q + 1)],
        )


def regroup_for_aggregation(nc, side_pool, raw, vector_d):
    side = side_pool.tile([P, PIECE_D, PACK], BF16, tag="side", align_bytes=64)
    dst = side[:].rearrange("p (c i) j -> p c j i", i=4)
    src = raw[:].rearrange("p (j c i) -> p c j i", j=PACK, i=4)
    cut = vector_d // 4
    nc.vector.tensor_copy(out=dst[:, 0:cut], in_=src[:, 0:cut])
    nc.scalar.copy(out=dst[:, cut:], in_=src[:, cut:])
    return side


def tile_netxtvladconsensus_pa_k_kernel(tc, xe, Ws, bn1_g, bn1_b, att_lin, ba, centroids, out):
    nc = tc.nc
    with ExitStack() as ctx:
        keep = ctx.enter_context(tc.tile_pool(name="keep", bufs=1))
        psum_acc = ctx.enter_context(tc.psum_pool(name="psum_acc", bufs=4))
        psum_tmp = ctx.enter_context(tc.psum_pool(name="psum_tmp", bufs=4))
        lo, hi = slice(0, P // 2), slice(P // 2, P)

        identity = keep.tile([P, P], F32)
        make_identity(nc, identity[:])
        ones = keep.tile([P, 2], F32)
        nc.vector.memset(ones[:], 1.0)
        minus_half = keep.tile([P, 1], F32)
        nc.vector.memset(minus_half[:], -0.5)
        table_warm = keep.tile([P, 1], F32)
        nc.scalar.activation(out=table_warm[:], in_=ones[:, 0:1], func=ACT.Exp)

        gb_rows = keep.tile([P, P], BF16)
        nc.vector.memset(gb_rows[:], 0.0)
        for row, vector in enumerate((bn1_g, bn1_b)):
            for cols in (lo, hi):
                nc.scalar.dma_start(out=gb_rows[row : row + 1, cols], in_=vector.rearrange("(o c) -> o c", o=1))
        att_raw = keep.tile([P, CLIPS, GROUPS], BF16)
        nc.scalar.dma_start(out=att_raw[:], in_=att_lin.rearrange("b l g -> l b g"))
        ba_all = keep.tile([P, GROUPS], BF16)
        nc.scalar.dma_start(out=ba_all[:], in_=ba.partition_broadcast(P))

        agg_codes = keep.tile([P, CLIPS, GROUP_HALVES, GROUP_WIDTH], U32, align_bytes=64)
        agg_scales = keep.tile([P, CLIPS, GROUP_HALVES, GROUP_WIDTH], U8, align_bytes=64)
        act_codes = keep.tile([P, CLIPS * GROUP_HALVES * P], U32, align_bytes=64)
        act_scales = keep.tile([P, CLIPS * GROUP_HALVES * P], U8, align_bytes=64)
        nc.vector.memset(act_codes[:].bitcast(I32), 0)
        nc.vector.memset(act_scales[:].bitcast(I32), 0)
        act_codes_v = act_codes[:].rearrange("p (b h m) -> p b h m", b=CLIPS, h=GROUP_HALVES)
        act_scales_v = act_scales[:].rearrange("p (b h m) -> p b h m", b=CLIPS, h=GROUP_HALVES)

        pair_sum = keep.tile([P, P], F32)
        pair_diff = keep.tile([P, P], F32)
        nc.vector.tensor_add(out=pair_sum[:, lo], in0=identity[:, lo], in1=identity[:, hi])
        nc.vector.tensor_add(out=pair_sum[:, hi], in0=identity[:, lo], in1=identity[:, hi])
        nc.vector.tensor_sub(out=pair_diff[:, lo], in0=identity[:, lo], in1=identity[:, hi])
        nc.vector.tensor_sub(out=pair_diff[:, hi], in0=identity[:, hi], in1=identity[:, lo])

        gb_rows32 = keep.tile([P, P], F32)
        nc.vector.tensor_copy(out=gb_rows32[:], in_=gb_rows[:])
        gb_ps = psum_tmp.tile([P, P], F32, tag="tmp")
        nc.tensor.transpose(gb_ps[:], gb_rows32[:], identity[:])
        gains = keep.tile([P, 2], F32)
        nc.vector.tensor_copy(out=gains[:, 0:1], in_=gb_ps[:, 0:1])
        nc.vector.tensor_scalar_mul(out=gains[:, 1:2], in0=gb_ps[:, 0:1], scalar1=-1.0)
        bn_bias = keep.tile([P, 1], F32)
        nc.vector.tensor_copy(out=bn_bias[:], in_=gb_ps[:, 1:2])

        att = keep.tile([P, CLIPS, GROUPS], F32)
        nc.vector.tensor_tensor(
            out=att[:], in0=att_raw[:], in1=ba_all[:].unsqueeze(1).to_broadcast([P, CLIPS, GROUPS]), op=ALU.add
        )
        nc.scalar.activation(out=att[:], in_=att[:], func=ACT.Exp, scale=-1.0)
        nc.vector.tensor_scalar_add(out=att[:], in0=att[:], scalar1=1.0)
        nc.vector.reciprocal(out=att[:], in_=att[:])

        stats = keep.tile([P, LOGIT_TILES, 6], F32)

        logits_t = [psum_acc.tile([P, ROWS], F32, tag="acc", name="logits_t%d" % i) for i in range(LOGIT_TILES)]

        pieces = [("x", 0, clip) for clip in range(CLIPS)]
        for chunk in range(CHUNKS):
            for i in range(LOGIT_TILES):
                pieces.append(("w", chunk, i))
                if chunk + 1 < CHUNKS:
                    pieces.append(("x", chunk + 1, i))

        def kind_of(number):
            return pieces[number][0] if 0 <= number < len(pieces) else "none"

        with ExitStack() as stream:
            stream.enter_context(tc.manual_schedule())
            raw_pool = stream.enter_context(tc.tile_pool(name="raw", bufs=6))
            grouped_pool = stream.enter_context(tc.tile_pool(name="grouped", bufs=3))
            side_pool = stream.enter_context(tc.tile_pool(name="side", bufs=2))
            frames_pool = stream.enter_context(tc.tile_pool(name="frames", bufs=2))
            weights_pool = stream.enter_context(tc.tile_pool(name="weights", bufs=4))
            raws, groupeds, sides, frame_ops, weight_ops = {}, {}, {}, {}, {}

            def multiply(number, passes):
                chunk, index = pieces[number][1:]
                w_codes, w_scales = weight_ops[number]
                x_codes, x_scales = frame_ops[chunk]
                for k in passes:
                    nc.tensor.matmul_mx(
                        out=logits_t[index][:],
                        lhsT=w_codes[:, P * k : P * (k + 1)].bitcast(FP8X4),
                        lhsT_scale=w_scales[:, P * k : P * (k + 1)],
                        rhs=x_codes[:, k, :].bitcast(FP8X4),
                        rhs_scale=x_scales[:, k, :],
                        start=(chunk == 0 and k == 0),
                        stop=(chunk == CHUNKS - 1 and k == PIECE_PASSES - 1),
                    )

            for step in range(len(pieces) + 4):
                if kind_of(step) != "none":
                    kind, chunk, index = pieces[step]
                    rows = xe[index] if kind == "x" else Ws[P * index : P * (index + 1), :]
                    raws[step] = load_piece(nc, raw_pool, rows, chunk)
                    groupeds[step] = transpose_piece(nc, psum_tmp, grouped_pool, identity, raws[step])
                if kind_of(step - 1) == "x":
                    chunk, index = pieces[step - 1][1:]
                    if index == 0:
                        x_codes = frames_pool.tile([P, PIECE_PASSES, ROWS], U32, tag="x_codes", align_bytes=64)
                        x_scales = frames_pool.tile([P, PIECE_PASSES, ROWS], U8, tag="x_scales", align_bytes=64)
                        frame_ops[chunk] = (x_codes, x_scales)
                    quantise_frames(nc, groupeds[step - 1], frame_ops[chunk][0], frame_ops[chunk][1], index)
                if kind_of(step - 1) == "w":
                    w_codes = weights_pool.tile([P, PIECE_PASSES * P], U32, tag="w_codes", align_bytes=64)
                    w_scales = weights_pool.tile([P, PIECE_PASSES * P], U8, tag="w_scales", align_bytes=64)
                    weight_ops[step - 1] = (w_codes, w_scales)
                    quantise_weights(nc, groupeds[step - 1], w_codes, w_scales)
                if kind_of(step - 3) == "w":
                    multiply(step - 3, range(PIECE_PASSES // 2, PIECE_PASSES))
                if kind_of(step - 2) == "w":
                    multiply(step - 2, range(PIECE_PASSES // 2))
                if kind_of(step - 1) == "x" and pieces[step - 1][1] != LATE_CHUNK:
                    sides[step - 1] = regroup_for_aggregation(nc, side_pool, raws[step - 1], VECTOR_D)
                if kind_of(step - 2) == "x" and pieces[step - 2][1] != LATE_CHUNK:
                    chunk, index = pieces[step - 2][1:]
                    half, part = divmod(chunk, D_PARTS)
                    d_cols = slice(PIECE_D * part, PIECE_D * (part + 1))
                    nc.vector.quantize_mx(
                        out=agg_codes[:, index, half, d_cols].bitcast(FP8X4),
                        scales=agg_scales[:, index, half, d_cols],
                        in_=sides[step - 2][:].rearrange("p d j -> p (d j)"),
                    )
                if kind_of(step - 4) == "w" and pieces[step - 4][1] == CHUNKS - 1:
                    index = pieces[step - 4][2]
                    nc.vector.bn_stats(out=stats[:, index, :], in_=logits_t[index][:])

        late_raw_pool = ctx.enter_context(tc.tile_pool(name="late_raw", bufs=CLIPS))
        late_side_pool = ctx.enter_context(tc.tile_pool(name="late_side", bufs=2))
        late_raws = [load_piece(nc, late_raw_pool, xe[clip], LATE_CHUNK) for clip in range(CLIPS)]
        tail = ctx.enter_context(tc.tile_pool(name="tail", bufs=4))

        cent = tail.tile([P, GROUP_WIDTH], BF16, bufs=1)
        nc.sync.dma_start(out=cent[lo, :], in_=centroids)
        nc.scalar.dma_start(out=cent[hi, :], in_=centroids)

        mean_var = tail.tile([P, 2], F32)
        nc.vector.bn_aggr(out=mean_var[:], in_=stats[:].rearrange("p i s -> p (i s)"))
        both_ps = psum_tmp.tile([P, 4], F32, tag="tmp")
        nc.tensor.matmul(both_ps[:, 0:2], lhsT=pair_sum[:], rhs=mean_var[:], start=True, stop=True)
        nc.tensor.matmul(both_ps[:, 2:4], lhsT=pair_diff[:], rhs=mean_var[:], start=True, stop=True)
        halves = tail.tile([P, 4], F32)
        nc.vector.tensor_scalar_mul(out=halves[:], in0=both_ps[:], scalar1=0.5)
        variance = tail.tile([P, 1], F32)
        nc.vector.scalar_tensor_tensor(
            out=variance[:], in0=halves[:, 2:3], scalar=halves[:, 2:3], in1=halves[:, 1:2], op0=ALU.mult, op1=ALU.add
        )
        nc.vector.tensor_scalar_add(out=variance[:], in0=variance[:], scalar1=EPS_BN)
        rstd = tail.tile([P, 1], F32)
        nc.gpsimd.tensor_tensor(out=rstd[:], in0=variance[:], in1=minus_half[:], op=ALU.pow)
        slopes = tail.tile([P, 2], F32)
        nc.vector.tensor_scalar_mul(out=slopes[:], in0=gains[:], scalar1=rstd[:, 0:1])
        shift = tail.tile([P, 1], F32)
        nc.vector.scalar_tensor_tensor(
            out=shift[:], in0=halves[:, 0:1], scalar=slopes[:, 1:2], in1=bn_bias[:], op0=ALU.mult, op1=ALU.add
        )
        normed_t = []
        for i in range(LOGIT_TILES):
            normed = tail.tile([P, ROWS], F32, name="normed%d" % i, bufs=1)
            if i % 2 == 0:
                nc.scalar.activation(
                    out=normed[:], in_=logits_t[i][:], func=ACT.Identity, bias=shift[:, 0:1], scale=slopes[:, 0:1]
                )
            else:
                nc.vector.tensor_scalar(
                    out=normed[:], in0=logits_t[i][:], scalar1=slopes[:, 0:1], scalar2=shift[:, 0:1],
                    op0=ALU.mult, op1=ALU.add,
                )
            normed_t.append(normed)

        z_banks = []
        for clip in range(CLIPS):
            z = psum_tmp.tile([P, LOGIT_TILES, P], F32, tag="tmp", name="z%d" % clip)
            for i in range(LOGIT_TILES):
                nc.tensor.transpose(z[:, i, :], normed_t[i][:, P * clip : P * (clip + 1)], identity[:])
            z_banks.append(z)

        firsts = [
            [psum_acc.tile([P, BANK], F32, tag="acc", name="first0_%d" % n) for n in range(D_BANKS)],
            [psum_tmp.tile([P, BANK], F32, tag="tmp", name="first1_%d" % n) for n in range(D_BANKS)],
        ]
        frame_sums = [tail.tile([P, P], F32, name="frame_sums%d" % pair, bufs=1) for pair in range(CLIPS // 2)]

        def softmax_and_gate(clip):
            pair, side_of_pair = divmod(clip, 2)
            cols = slice(CLUSTERS * side_of_pair, CLUSTERS * (side_of_pair + 1))
            z_gc = z_banks[clip][:].rearrange("p i k -> p (i k)").rearrange("p (c g) -> p g c", g=GROUPS)
            neg_max = tail.tile([P, GROUPS], F32, tag="neg_max")
            nc.vector.tensor_reduce(out=neg_max[:], in_=z_gc, axis=AXIS.X, op=ALU.max, negate=True)
            expo = tail.tile([P, GROUPS, CLUSTERS], F32, tag="expo")
            sums = tail.tile([P, GROUPS], F32, tag="sums")
            for g in range(GROUPS):
                nc.scalar.activation(
                    out=expo[:, g, :], in_=z_gc[:, g, :], func=ACT.Exp, bias=neg_max[:, g : g + 1], scale=1.0,
                    accum_out=sums[:, g : g + 1],
                )
            weight = tail.tile([P, GROUPS], F32, tag="weight")
            nc.vector.reciprocal(out=weight[:], in_=sums[:])
            nc.vector.tensor_mul(out=weight[:], in0=weight[:], in1=att[:, clip, :])
            act16 = tail.tile([P, GROUP_HALVES, CLUSTERS, PACK], BF16, tag="act16", align_bytes=64)
            nc.vector.tensor_tensor(
                out=act16[:],
                in0=expo[:].rearrange("p (h j) c -> p h c j", j=PACK),
                in1=weight[:].rearrange("p (h j) -> p h j", j=PACK).unsqueeze(2).to_broadcast(
                    [P, GROUP_HALVES, CLUSTERS, PACK]
                ),
                op=ALU.mult,
            )
            for half in range(GROUP_HALVES):
                nc.vector.quantize_mx(
                    out=act_codes_v[:, clip, half, cols].bitcast(FP8X4),
                    scales=act_scales_v[:, clip, half, cols],
                    in_=act16[:, half].rearrange("p c j -> p (c j)"),
                )
            act32 = tail.tile([P, GROUPS, CLUSTERS], F32, tag="act32")
            nc.gpsimd.tensor_tensor(
                out=act32[:], in0=expo[:], in1=weight[:].unsqueeze(2).to_broadcast([P, GROUPS, CLUSTERS]), op=ALU.mult
            )
            nc.gpsimd.tensor_tensor(out=act32[:, 0:4, :], in0=act32[:, 0:4, :], in1=act32[:, 4:8, :], op=ALU.add)
            nc.gpsimd.tensor_tensor(out=act32[:, 0:2, :], in0=act32[:, 0:2, :], in1=act32[:, 2:4, :], op=ALU.add)
            nc.gpsimd.tensor_tensor(out=frame_sums[pair][:, cols], in0=act32[:, 0, :], in1=act32[:, 1, :], op=ALU.add)

        def aggregate(clip):
            pair, side_of_pair = divmod(clip, 2)
            for n in range(D_BANKS):
                for half in range(GROUP_HALVES):
                    nc.tensor.matmul_mx(
                        out=firsts[pair][n][:],
                        lhsT=act_codes_v[:, clip, half, :].bitcast(FP8X4),
                        lhsT_scale=act_scales_v[:, clip, half, :],
                        rhs=agg_codes[:, clip, half, BANK * n : BANK * (n + 1)].bitcast(FP8X4),
                        rhs_scale=agg_scales[:, clip, half, BANK * n : BANK * (n + 1)],
                        start=(side_of_pair == 0 and half == 0),
                        stop=(side_of_pair == 1 and half == GROUP_HALVES - 1),
                    )

        def sum_over_frames(pair, small_pool, small_tag):
            a_ps = small_pool.tile([P, 2], F32, tag=small_tag, name="a_ps%d" % pair)
            nc.tensor.matmul(a_ps[:], lhsT=frame_sums[pair][:], rhs=ones[:], start=True, stop=True)
            return a_ps

        def quantise_late_piece(clip):
            half, part = divmod(LATE_CHUNK, D_PARTS)
            side = regroup_for_aggregation(nc, late_side_pool, late_raws[clip], LATE_VECTOR_D)
            width = PIECE_D // 2
            for piece_half in range(2):
                d_cols = slice(PIECE_D * part + width * piece_half, PIECE_D * part + width * (piece_half + 1))
                nc.vector.quantize_mx(
                    out=agg_codes[:, clip, half, d_cols].bitcast(FP8X4),
                    scales=agg_scales[:, clip, half, d_cols],
                    in_=side[:, width * piece_half : width * (piece_half + 1), :].rearrange("p d j -> p (d j)"),
                )

        a_sums = []
        for clip in range(CLIPS):
            softmax_and_gate(clip)
            quantise_late_piece(clip)
            aggregate(clip)
            if clip == 1:
                a_sums.append(sum_over_frames(0, psum_tmp, "tmp"))
            if clip == 3:
                a_sums.append(sum_over_frames(1, psum_acc, "acc"))

        out_rows = out.rearrange("b c d -> (b c) d")
        for pair in range(CLIPS // 2):
            neg_a = tail.tile([P, 1], F32, tag="neg_a")
            nc.vector.tensor_scalar_mul(out=neg_a[:], in0=a_sums[pair][:, 0:1], scalar1=-1.0)
            vlad = tail.tile([P, GROUP_WIDTH], F32, tag="vlad")
            squares = tail.tile([P, D_BANKS], F32, tag="squares")
            for n in range(D_BANKS):
                d_cols = slice(BANK * n, BANK * (n + 1))
                nc.vector.scalar_tensor_tensor(
                    out=vlad[:, d_cols], in0=cent[:, d_cols], scalar=neg_a[:, 0:1], in1=firsts[pair][n][:],
                    op0=ALU.mult, op1=ALU.add,
                )
                squared = tail.tile([P, BANK], F32, tag="squared")
                nc.scalar.activation(
                    out=squared[:], in_=vlad[:, d_cols], func=ACT.Square, accum_out=squares[:, n : n + 1]
                )
            norm2 = tail.tile([P, 1], F32, tag="norm2")
            nc.vector.tensor_reduce(out=norm2[:], in_=squares[:], axis=AXIS.X, op=ALU.add)
            nc.vector.tensor_scalar_max(out=norm2[:], in0=norm2[:], scalar1=EPS_L2 * EPS_L2)
            inv_norm = tail.tile([P, 1], F32, tag="inv_norm")
            nc.gpsimd.tensor_tensor(out=inv_norm[:], in0=norm2[:], in1=minus_half[:], op=ALU.pow)
            left, right = slice(0, GROUP_WIDTH // 2), slice(GROUP_WIDTH // 2, GROUP_WIDTH)
            nc.vector.tensor_scalar_mul(out=vlad[:, left], in0=vlad[:, left], scalar1=inv_norm[:, 0:1])
            nc.sync.dma_start(out=out_rows[P * pair : P * (pair + 1), left], in_=vlad[:, left])
            nc.scalar.activation(out=vlad[:, right], in_=vlad[:, right], func=ACT.Copy, scale=inv_norm[:, 0:1])
            nc.sync.dma_start(out=out_rows[P * pair : P * (pair + 1), right], in_=vlad[:, right])
